import numpy as np
import ml_dtypes

BF16 = ml_dtypes.bfloat16


def bf(x):
    return np.asarray(x, np.float32).astype(BF16)


def f32(x):
    return np.asarray(x, np.float32)


def f64(x):
    return np.asarray(x).astype(np.float64)


def striped(idx):
    return np.tile(idx.reshape(-1, 16).T, (8, 1))


C, S, N, M = 128, 2048, 1024, 384
EPS = 1e-5


def setup_inputs():
    return {
        "embed": f32(np.random.standard_normal((C, S))),
        "pos": f32(0.5 * np.random.standard_normal((C, N))),
        "ln_w": f32(1.0 + 0.1 * np.random.standard_normal((C, 1))),
        "ln_b": f32(0.1 * np.random.standard_normal((C, 1))),
        "w_attn": bf(np.random.standard_normal((C, M)) / np.sqrt(C)),
        "b_attn": f32(0.1 * np.random.standard_normal((M, 1))),
        "offs": striped(np.random.permutation(np.tile(np.arange(S), 2))[:N]),
    }


def reference(embed, pos, ln_w, ln_b, w_attn, b_attn, offs):
    idx = offs[:16].T.reshape(-1)
    res = f64(embed)[:, idx] + f64(pos)
    mean = res.mean(axis=0, keepdims=True)
    std = np.sqrt(((res - mean) ** 2).mean(axis=0, keepdims=True))
    x = f64(ln_w) * ((res - mean) / (std + EPS)) + f64(ln_b)
    qkv = f64(w_attn).T @ x + f64(b_attn)
    return np.concatenate([res, qkv], axis=0)

@@ -1,0 +1,113 @@
+import concourse.mybir as mybir
+from concourse.masks import make_identity
+
+F32 = mybir.dt.float32
+BF16 = mybir.dt.bfloat16
+U16 = mybir.dt.uint16
+ADD = mybir.AluOpType.add
+SUBTRACT = mybir.AluOpType.subtract
+MULT = mybir.AluOpType.mult
+SQRT = mybir.ActivationFunctionType.Sqrt
+IDENTITY = mybir.ActivationFunctionType.Identity
+
+C = 128
+WORDS = 2048
+TOKENS = 1024
+M_BLOCKS = 3
+EPS = 1e-5
+
+BLOCK = 128
+CHUNK = 256
+BLOCKS = CHUNK // BLOCK
+CHUNKS = TOKENS // CHUNK
+OFFSET_COLUMNS = CHUNK // 16
+
+FLOPS = 2 * C * M_BLOCKS * 128 * TOKENS
+
+
+def tile_jtransformer_kernel(tc, embed, pos, ln_w, ln_b, w_attn, b_attn, offs, out):
+    nc = tc.nc
+    with (
+        tc.tile_pool(name="held", bufs=1) as held,
+        tc.tile_pool(name="work", bufs=2) as work,
+        tc.tile_pool(name="stores", bufs=4) as stores,
+        tc.psum_pool(name="psum_flip", bufs=2) as psum_flip,
+        tc.psum_pool(name="psum_qkv", bufs=4) as psum_qkv,
+    ):
+        offsets = held.tile([C, TOKENS // 16], U16, name="offsets")
+        nc.sync.dma_start(offsets[:], offs)
+        table = held.tile([C, WORDS], F32, name="table")
+        nc.sync.dma_start(table[:, : WORDS // 2], embed[:, : WORDS // 2])
+        nc.scalar.dma_start(table[:, WORDS // 2 :], embed[:, WORDS // 2 :])
+        positions = []
+        for k in range(CHUNKS):
+            pos_k = held.tile([C, CHUNK], F32, name=f"pos{k}")
+            nc.sync.dma_start(pos_k[:], pos[:, k * CHUNK : (k + 1) * CHUNK])
+            positions.append(pos_k)
+        weights = held.tile([C, M_BLOCKS * 128], BF16, name="weights")
+        nc.scalar.dma_start(weights[:], w_attn)
+        gain = held.tile([C, 1], F32, name="gain")
+        nc.scalar.dma_start(gain[:], ln_w)
+        shift = held.tile([C, 1], F32, name="shift")
+        nc.scalar.dma_start(shift[:], ln_b)
+        biases = []
+        for m in range(M_BLOCKS):
+            bias_m = held.tile([128, 1], F32, name=f"bias{m}")
+            nc.scalar.dma_start(bias_m[:], b_attn[m * 128 : (m + 1) * 128, :])
+            biases.append(bias_m)
+        identity = held.tile([128, 128], F32, name="identity")
+        make_identity(nc, identity[:])
+
+        for k in range(CHUNKS):
+            columns = slice(k * CHUNK, (k + 1) * CHUNK)
+
+            res = stores.tile([C, CHUNK], F32, name="res")
+            nc.vector.tensor_tensor(
+                res[:],
+                table[:].indirect(offsets[:, k * OFFSET_COLUMNS : (k + 1) * OFFSET_COLUMNS]),
+                positions[k][:],
+                ADD,
+            )
+            nc.sync.dma_start(out[0:C, columns], res[:])
+
+            res_t = psum_flip.tile([BLOCK, BLOCKS * C], F32, name="res_t")
+            for b in range(BLOCKS):
+                nc.tensor.transpose(res_t[:, b * C : (b + 1) * C], res[:, b * BLOCK : (b + 1) * BLOCK], identity[:])
+
+            stats = work.tile([BLOCK, BLOCKS, 6], F32, name="stats")
+            mean_var = work.tile([BLOCK, BLOCKS, 2], F32, name="mean_var")
+            for b in range(BLOCKS):
+                nc.vector.bn_stats(stats[:, b, :], res_t[:, b * C : (b + 1) * C])
+                nc.vector.bn_aggr(mean_var[:, b, :], stats[:, b, :])
+
+            std = work.tile([BLOCK, BLOCKS, 1], F32, name="std")
+            nc.scalar.activation(std[:], mean_var[:, :, 1:2], SQRT)
+            nc.vector.tensor_scalar_add(std[:], std[:], EPS)
+            inv_std = work.tile([BLOCK, BLOCKS, 1], F32, name="inv_std")
+            nc.vector.reciprocal(inv_std[:], std[:])
+
+            normed = work.tile([BLOCK, BLOCKS * C], F32, name="normed")
+            for b in range(BLOCKS):
+                nc.vector.tensor_scalar(
+                    normed[:, b * C : (b + 1) * C],
+                    res_t[:, b * C : (b + 1) * C],
+                    mean_var[:, b, 0:1],
+                    inv_std[:, b, :],
+                    SUBTRACT,
+                    MULT,
+                )
+
+            normed_t = psum_flip.tile([C, CHUNK], F32, name="normed_t")
+            for b in range(BLOCKS):
+                nc.tensor.transpose(
+                    normed_t[:, b * BLOCK : (b + 1) * BLOCK], normed[:, b * C : (b + 1) * C], identity[:]
+                )
+            x = work.tile([C, CHUNK], BF16, name="x")
+            nc.scalar.activation(x[:], normed_t[:], IDENTITY, bias=shift[:], scale=gain[:])
+
+            for m in range(M_BLOCKS):
+                product = psum_qkv.tile([128, CHUNK], F32, name="product")
+                nc.tensor.matmul(product[:], weights[:, m * 128 : (m + 1) * 128], x[:], start=True, stop=True)
+                qkv = stores.tile([128, CHUNK], F32, name="qkv")
+                nc.scalar.activation(qkv[:], product[:], IDENTITY, bias=biases[m][:])
+                nc.sync.dma_start(out[C + m * 128 : C + (m + 1) * 128, columns], qkv[:])

@@ -21,6 +21,8 @@ CHUNK = 256
 BLOCKS = CHUNK // BLOCK
 CHUNKS = TOKENS // CHUNK
 OFFSET_COLUMNS = CHUNK // 16
+PSUM_BANKS = 8
+TABLE_LOADS = 4
 
 FLOPS = 2 * C * M_BLOCKS * 128 * TOKENS
 
@@ -29,51 +31,54 @@ def tile_jtransformer_kernel(tc, embed, pos, ln_w, ln_b, w_attn, b_attn, offs, o
     nc = tc.nc
     with (
         tc.tile_pool(name="held", bufs=1) as held,
-        tc.tile_pool(name="work", bufs=2) as work,
-        tc.tile_pool(name="stores", bufs=4) as stores,
-        tc.psum_pool(name="psum_flip", bufs=2) as psum_flip,
-        tc.psum_pool(name="psum_qkv", bufs=4) as psum_qkv,
+        tc.tile_pool(name="work", bufs=CHUNKS) as work,
+        tc.psum_pool(name="psum", bufs=PSUM_BANKS) as psum,
     ):
         offsets = held.tile([C, TOKENS // 16], U16, name="offsets")
         nc.sync.dma_start(offsets[:], offs)
         table = held.tile([C, WORDS], F32, name="table")
-        nc.sync.dma_start(table[:, : WORDS // 2], embed[:, : WORDS // 2])
-        nc.scalar.dma_start(table[:, WORDS // 2 :], embed[:, WORDS // 2 :])
+        for q in range(TABLE_LOADS):
+            words = slice(q * WORDS // TABLE_LOADS, (q + 1) * WORDS // TABLE_LOADS)
+            nc.sync.dma_start(table[:, words], embed[:, words])
         positions = []
         for k in range(CHUNKS):
             pos_k = held.tile([C, CHUNK], F32, name=f"pos{k}")
             nc.sync.dma_start(pos_k[:], pos[:, k * CHUNK : (k + 1) * CHUNK])
             positions.append(pos_k)
         weights = held.tile([C, M_BLOCKS * 128], BF16, name="weights")
-        nc.scalar.dma_start(weights[:], w_attn)
-        gain = held.tile([C, 1], F32, name="gain")
-        nc.scalar.dma_start(gain[:], ln_w)
-        shift = held.tile([C, 1], F32, name="shift")
-        nc.scalar.dma_start(shift[:], ln_b)
-        biases = []
-        for m in range(M_BLOCKS):
-            bias_m = held.tile([128, 1], F32, name=f"bias{m}")
-            nc.scalar.dma_start(bias_m[:], b_attn[m * 128 : (m + 1) * 128, :])
-            biases.append(bias_m)
+        nc.sync.dma_start(weights[:], w_attn)
         identity = held.tile([128, 128], F32, name="identity")
         make_identity(nc, identity[:])
+        gain = held.tile([C, 1], F32, name="gain")
+        nc.sync.dma_start(gain[:], ln_w)
+        shift = held.tile([C, 1], F32, name="shift")
+        nc.sync.dma_start(shift[:], ln_b)
+        bias = held.tile([128, M_BLOCKS], F32, name="bias")
+        with nc.allow_non_contiguous_dma(reason="384 single values, one to a partition and block"):
+            nc.sync.dma_start(bias[:], b_attn.rearrange("(m p) one -> p (m one)", p=128))
 
+        one = held.tile([128, 1], F32, name="one")
+        nc.vector.memset(one[:], 1.0)
+        nc.scalar.activation(one[:], one[:], SQRT)
+
+        res_ts = []
         for k in range(CHUNKS):
-            columns = slice(k * CHUNK, (k + 1) * CHUNK)
-
-            res = stores.tile([C, CHUNK], F32, name="res")
+            res = work.tile([C, CHUNK], F32, name="res")
             nc.vector.tensor_tensor(
                 res[:],
                 table[:].indirect(offsets[:, k * OFFSET_COLUMNS : (k + 1) * OFFSET_COLUMNS]),
                 positions[k][:],
                 ADD,
             )
-            nc.sync.dma_start(out[0:C, columns], res[:])
-
-            res_t = psum_flip.tile([BLOCK, BLOCKS * C], F32, name="res_t")
+            nc.sync.dma_start(out[0:C, k * CHUNK : (k + 1) * CHUNK], res[:])
+            res_t = psum.tile([BLOCK, BLOCKS * C], F32, name="res_t", tag="bank")
             for b in range(BLOCKS):
                 nc.tensor.transpose(res_t[:, b * C : (b + 1) * C], res[:, b * BLOCK : (b + 1) * BLOCK], identity[:])
+            res_ts.append(res_t)
 
+        xs = []
+        for k in range(CHUNKS):
+            res_t = res_ts[k]
             stats = work.tile([BLOCK, BLOCKS, 6], F32, name="stats")
             mean_var = work.tile([BLOCK, BLOCKS, 2], F32, name="mean_var")
             for b in range(BLOCKS):
@@ -97,17 +102,22 @@ def tile_jtransformer_kernel(tc, embed, pos, ln_w, ln_b, w_attn, b_attn, offs, o
                     MULT,
                 )
 
-            normed_t = psum_flip.tile([C, CHUNK], F32, name="normed_t")
+            normed_t = psum.tile([C, CHUNK], F32, name="normed_t", tag="bank")
             for b in range(BLOCKS):
                 nc.tensor.transpose(
                     normed_t[:, b * BLOCK : (b + 1) * BLOCK], normed[:, b * C : (b + 1) * C], identity[:]
                 )
             x = work.tile([C, CHUNK], BF16, name="x")
             nc.scalar.activation(x[:], normed_t[:], IDENTITY, bias=shift[:], scale=gain[:])
+            xs.append(x)
 
+        for k in range(CHUNKS):
             for m in range(M_BLOCKS):
-                product = psum_qkv.tile([128, CHUNK], F32, name="product")
-                nc.tensor.matmul(product[:], weights[:, m * 128 : (m + 1) * 128], x[:], start=True, stop=True)
-                qkv = stores.tile([128, CHUNK], F32, name="qkv")
-                nc.scalar.activation(qkv[:], product[:], IDENTITY, bias=biases[m][:])
-                nc.sync.dma_start(out[C + m * 128 : C + (m + 1) * 128, columns], qkv[:])
+                product = psum.tile([128, CHUNK], F32, name="product", tag="bank")
+                nc.tensor.matmul(product[:], weights[:, m * 128 : (m + 1) * 128], xs[k][:], start=True, stop=True)
+                qkv = work.tile([128, CHUNK], F32, name=f"qkv{m}")
+                if (k * M_BLOCKS + m) % 2 == 0:
+                    nc.scalar.activation(qkv[:], product[:], IDENTITY, bias=bias[:, m : m + 1])
+                else:
+                    nc.vector.tensor_scalar_add(qkv[:], product[:], bias[:, m : m + 1])
+                nc.sync.dma_start(out[C + m * 128 : C + (m + 1) * 128, k * CHUNK : (k + 1) * CHUNK], qkv[:])

@@ -17,10 +17,10 @@ M_BLOCKS = 3
 EPS = 1e-5
 
 BLOCK = 128
-CHUNK = 256
-BLOCKS = CHUNK // BLOCK
-CHUNKS = TOKENS // CHUNK
-OFFSET_COLUMNS = CHUNK // 16
+CHUNK_TOKENS = [128, 256, 256, 256, 128]
+CHUNKS = len(CHUNK_TOKENS)
+CHUNK_STARTS = [sum(CHUNK_TOKENS[:k]) for k in range(CHUNKS)]
+LAG = 1
 PSUM_BANKS = 8
 TABLE_LOADS = 4
 
@@ -42,8 +42,8 @@ def tile_jtransformer_kernel(tc, embed, pos, ln_w, ln_b, w_attn, b_attn, offs, o
             nc.sync.dma_start(table[:, words], embed[:, words])
         positions = []
         for k in range(CHUNKS):
-            pos_k = held.tile([C, CHUNK], F32, name=f"pos{k}")
-            nc.sync.dma_start(pos_k[:], pos[:, k * CHUNK : (k + 1) * CHUNK])
+            pos_k = held.tile([C, CHUNK_TOKENS[k]], F32, name=f"pos{k}")
+            nc.sync.dma_start(pos_k[:], pos[:, CHUNK_STARTS[k] : CHUNK_STARTS[k] + CHUNK_TOKENS[k]])
             positions.append(pos_k)
         weights = held.tile([C, M_BLOCKS * 128], BF16, name="weights")
         nc.sync.dma_start(weights[:], w_attn)
@@ -61,38 +61,35 @@ def tile_jtransformer_kernel(tc, embed, pos, ln_w, ln_b, w_attn, b_attn, offs, o
         nc.vector.memset(one[:], 1.0)
         nc.scalar.activation(one[:], one[:], SQRT)
 
-        res_ts = []
-        for k in range(CHUNKS):
-            res = work.tile([C, CHUNK], F32, name="res")
+        def look_up(k):
+            start, tokens = CHUNK_STARTS[k], CHUNK_TOKENS[k]
+            res = work.tile([C, tokens], F32, name="res")
             nc.vector.tensor_tensor(
-                res[:],
-                table[:].indirect(offsets[:, k * OFFSET_COLUMNS : (k + 1) * OFFSET_COLUMNS]),
-                positions[k][:],
-                ADD,
+                res[:], table[:].indirect(offsets[:, start // 16 : (start + tokens) // 16]), positions[k][:], ADD
             )
-            nc.sync.dma_start(out[0:C, k * CHUNK : (k + 1) * CHUNK], res[:])
-            res_t = psum.tile([BLOCK, BLOCKS * C], F32, name="res_t", tag="bank")
-            for b in range(BLOCKS):
+            nc.sync.dma_start(out[0:C, start : start + tokens], res[:])
+            res_t = psum.tile([BLOCK, tokens], F32, name="res_t", tag="bank")
+            for b in range(tokens // BLOCK):
                 nc.tensor.transpose(res_t[:, b * C : (b + 1) * C], res[:, b * BLOCK : (b + 1) * BLOCK], identity[:])
-            res_ts.append(res_t)
+            return res_t
 
-        xs = []
-        for k in range(CHUNKS):
-            res_t = res_ts[k]
-            stats = work.tile([BLOCK, BLOCKS, 6], F32, name="stats")
-            mean_var = work.tile([BLOCK, BLOCKS, 2], F32, name="mean_var")
-            for b in range(BLOCKS):
+        def layer_norm(k, res_t):
+            tokens = CHUNK_TOKENS[k]
+            blocks = tokens // BLOCK
+            stats = work.tile([BLOCK, blocks, 6], F32, name="stats")
+            mean_var = work.tile([BLOCK, blocks, 2], F32, name="mean_var")
+            for b in range(blocks):
                 nc.vector.bn_stats(stats[:, b, :], res_t[:, b * C : (b + 1) * C])
                 nc.vector.bn_aggr(mean_var[:, b, :], stats[:, b, :])
 
-            std = work.tile([BLOCK, BLOCKS, 1], F32, name="std")
+            std = work.tile([BLOCK, blocks, 1], F32, name="std")
             nc.scalar.activation(std[:], mean_var[:, :, 1:2], SQRT)
             nc.vector.tensor_scalar_add(std[:], std[:], EPS)
-            inv_std = work.tile([BLOCK, BLOCKS, 1], F32, name="inv_std")
+            inv_std = work.tile([BLOCK, blocks, 1], F32, name="inv_std")
             nc.vector.reciprocal(inv_std[:], std[:])
 
-            normed = work.tile([BLOCK, BLOCKS * C], F32, name="normed")
-            for b in range(BLOCKS):
+            normed = work.tile([BLOCK, tokens], F32, name="normed")
+            for b in range(blocks):
                 nc.vector.tensor_scalar(
                     normed[:, b * C : (b + 1) * C],
                     res_t[:, b * C : (b + 1) * C],
@@ -102,22 +99,31 @@ def tile_jtransformer_kernel(tc, embed, pos, ln_w, ln_b, w_attn, b_attn, offs, o
                     MULT,
                 )
 
-            normed_t = psum.tile([C, CHUNK], F32, name="normed_t", tag="bank")
-            for b in range(BLOCKS):
+            normed_t = psum.tile([C, tokens], F32, name="normed_t", tag="bank")
+            for b in range(blocks):
                 nc.tensor.transpose(
                     normed_t[:, b * BLOCK : (b + 1) * BLOCK], normed[:, b * C : (b + 1) * C], identity[:]
                 )
-            x = work.tile([C, CHUNK], BF16, name="x")
+            x = work.tile([C, tokens], BF16, name="x")
             nc.scalar.activation(x[:], normed_t[:], IDENTITY, bias=shift[:], scale=gain[:])
-            xs.append(x)
+            return x
 
-        for k in range(CHUNKS):
+        def project(k, x):
+            start, tokens = CHUNK_STARTS[k], CHUNK_TOKENS[k]
             for m in range(M_BLOCKS):
-                product = psum.tile([128, CHUNK], F32, name="product", tag="bank")
-                nc.tensor.matmul(product[:], weights[:, m * 128 : (m + 1) * 128], xs[k][:], start=True, stop=True)
-                qkv = work.tile([128, CHUNK], F32, name=f"qkv{m}")
-                if (k * M_BLOCKS + m) % 2 == 0:
+                product = psum.tile([128, tokens], F32, name="product", tag="bank")
+                nc.tensor.matmul(product[:], weights[:, m * 128 : (m + 1) * 128], x[:], start=True, stop=True)
+                qkv = work.tile([128, tokens], F32, name=f"qkv{m}")
+                if k < CHUNKS - 1 - LAG or (k * M_BLOCKS + m) % 2 == 0:
                     nc.scalar.activation(qkv[:], product[:], IDENTITY, bias=bias[:, m : m + 1])
                 else:
                     nc.vector.tensor_scalar_add(qkv[:], product[:], bias[:, m : m + 1])
-                nc.sync.dma_start(out[C + m * 128 : C + (m + 1) * 128, k * CHUNK : (k + 1) * CHUNK], qkv[:])
+                nc.sync.dma_start(out[C + m * 128 : C + (m + 1) * 128, start : start + tokens], qkv[:])
+
+        res_ts = [look_up(k) for k in range(CHUNKS)]
+        xs = []
+        for k in range(CHUNKS + LAG):
+            if k < CHUNKS:
+                xs.append(layer_norm(k, res_ts[k]))
+            if k >= LAG:
+                project(k - LAG, xs[k - LAG])

@@ -22,6 +22,7 @@ CHUNKS = len(CHUNK_TOKENS)
 CHUNK_STARTS = [sum(CHUNK_TOKENS[:k]) for k in range(CHUNKS)]
 LAG = 1
 PSUM_BANKS = 8
+DMA_ALIGN = 256
 TABLE_LOADS = 4
 
 FLOPS = 2 * C * M_BLOCKS * 128 * TOKENS
@@ -36,13 +37,13 @@ def tile_jtransformer_kernel(tc, embed, pos, ln_w, ln_b, w_attn, b_attn, offs, o
     ):
         offsets = held.tile([C, TOKENS // 16], U16, name="offsets")
         nc.sync.dma_start(offsets[:], offs)
-        table = held.tile([C, WORDS], F32, name="table")
+        table = held.tile([C, WORDS], F32, name="table", align_bytes=DMA_ALIGN)
         for q in range(TABLE_LOADS):
             words = slice(q * WORDS // TABLE_LOADS, (q + 1) * WORDS // TABLE_LOADS)
             nc.sync.dma_start(table[:, words], embed[:, words])
         positions = []
         for k in range(CHUNKS):
-            pos_k = held.tile([C, CHUNK_TOKENS[k]], F32, name=f"pos{k}")
+            pos_k = held.tile([C, CHUNK_TOKENS[k]], F32, name=f"pos{k}", align_bytes=DMA_ALIGN)
             nc.sync.dma_start(pos_k[:], pos[:, CHUNK_STARTS[k] : CHUNK_STARTS[k] + CHUNK_TOKENS[k]])
             positions.append(pos_k)
         weights = held.tile([C, M_BLOCKS * 128], BF16, name="weights")
@@ -63,7 +64,7 @@ def tile_jtransformer_kernel(tc, embed, pos, ln_w, ln_b, w_attn, b_attn, offs, o
 
         def look_up(k):
             start, tokens = CHUNK_STARTS[k], CHUNK_TOKENS[k]
-            res = work.tile([C, tokens], F32, name="res")
+            res = work.tile([C, tokens], F32, name="res", align_bytes=DMA_ALIGN)
             nc.vector.tensor_tensor(
                 res[:], table[:].indirect(offsets[:, start // 16 : (start + tokens) // 16]), positions[k][:], ADD
             )
@@ -113,7 +114,7 @@ def tile_jtransformer_kernel(tc, embed, pos, ln_w, ln_b, w_attn, b_attn, offs, o
             for m in range(M_BLOCKS):
                 product = psum.tile([128, tokens], F32, name="product", tag="bank")
                 nc.tensor.matmul(product[:], weights[:, m * 128 : (m + 1) * 128], x[:], start=True, stop=True)
-                qkv = work.tile([128, tokens], F32, name=f"qkv{m}")
+                qkv = work.tile([128, tokens], F32, name=f"qkv{m}", align_bytes=DMA_ALIGN)
                 if k < CHUNKS - 1 - LAG or (k * M_BLOCKS + m) % 2 == 0:
                     nc.scalar.activation(qkv[:], product[:], IDENTITY, bias=bias[:, m : m + 1])
                 else:

@@ -77,14 +77,15 @@ def tile_jtransformer_kernel(tc, embed, pos, ln_w, ln_b, w_attn, b_attn, offs, o
         def layer_norm(k, res_t):
             tokens = CHUNK_TOKENS[k]
             blocks = tokens // BLOCK
-            stats = work.tile([BLOCK, blocks, 6], F32, name="stats")
-            mean_var = work.tile([BLOCK, blocks, 2], F32, name="mean_var")
-            for b in range(blocks):
-                nc.vector.bn_stats(stats[:, b, :], res_t[:, b * C : (b + 1) * C])
-                nc.vector.bn_aggr(mean_var[:, b, :], stats[:, b, :])
+            stream = res_t[:].rearrange("t (b c) -> t c b", c=C)
+            if blocks == 1:
+                stream = stream.to_broadcast([BLOCK, C, 2])
+            stats = work.tile([BLOCK, 6], F32, name="stats")
+            nc.vector.bn_stats(stats[:], stream)
+            sets = stats[:].rearrange("t (b s) -> t b s", s=3)
 
             std = work.tile([BLOCK, blocks, 1], F32, name="std")
-            nc.scalar.activation(std[:], mean_var[:, :, 1:2], SQRT)
+            nc.scalar.activation(std[:], sets[:, 0:blocks, 2:3], SQRT, scale=1.0 / C)
             nc.vector.tensor_scalar_add(std[:], std[:], EPS)
             inv_std = work.tile([BLOCK, blocks, 1], F32, name="inv_std")
             nc.vector.reciprocal(inv_std[:], std[:])
@@ -94,7 +95,7 @@ def tile_jtransformer_kernel(tc, embed, pos, ln_w, ln_b, w_attn, b_attn, offs, o
                 nc.vector.tensor_scalar(
                     normed[:, b * C : (b + 1) * C],
                     res_t[:, b * C : (b + 1) * C],
-                    mean_var[:, b, 0:1],
+                    sets[:, b, 1:2],
                     inv_std[:, b, :],
                     SUBTRACT,
                     MULT,

@@ -116,7 +116,7 @@ def tile_jtransformer_kernel(tc, embed, pos, ln_w, ln_b, w_attn, b_attn, offs, o
                 product = psum.tile([128, tokens], F32, name="product", tag="bank")
                 nc.tensor.matmul(product[:], weights[:, m * 128 : (m + 1) * 128], x[:], start=True, stop=True)
                 qkv = work.tile([128, tokens], F32, name=f"qkv{m}", align_bytes=DMA_ALIGN)
-                if k < CHUNKS - 1 - LAG or (k * M_BLOCKS + m) % 2 == 0:
+                if (k * M_BLOCKS + m) % 2 == 0:
                     nc.scalar.activation(qkv[:], product[:], IDENTITY, bias=bias[:, m : m + 1])
                 else:
                     nc.vector.tensor_scalar_add(qkv[:], product[:], bias[:, m : m + 1])

@@ -17,9 +17,12 @@ M_BLOCKS = 3
 EPS = 1e-5
 
 BLOCK = 128
-CHUNK_TOKENS = [128, 256, 256, 256, 128]
-CHUNKS = len(CHUNK_TOKENS)
-CHUNK_STARTS = [sum(CHUNK_TOKENS[:k]) for k in range(CHUNKS)]
+BLOCKS = TOKENS // BLOCK
+PAIR = 2
+EPS_COLUMN = 8
+PIECE_BLOCKS = [1, 2, 2, 2, 1]
+PIECES = len(PIECE_BLOCKS)
+PIECE_STARTS = [sum(PIECE_BLOCKS[:k]) for k in range(PIECES)]
 LAG = 1
 PSUM_BANKS = 8
 DMA_ALIGN = 256
@@ -32,7 +35,7 @@ def tile_jtransformer_kernel(tc, embed, pos, ln_w, ln_b, w_attn, b_attn, offs, o
     nc = tc.nc
     with (
         tc.tile_pool(name="held", bufs=1) as held,
-        tc.tile_pool(name="work", bufs=CHUNKS) as work,
+        tc.tile_pool(name="work", bufs=PIECES) as work,
         tc.psum_pool(name="psum", bufs=PSUM_BANKS) as psum,
     ):
         offsets = held.tile([C, TOKENS // 16], U16, name="offsets")
@@ -42,10 +45,10 @@ def tile_jtransformer_kernel(tc, embed, pos, ln_w, ln_b, w_attn, b_attn, offs, o
             words = slice(q * WORDS // TABLE_LOADS, (q + 1) * WORDS // TABLE_LOADS)
             nc.sync.dma_start(table[:, words], embed[:, words])
         positions = []
-        for k in range(CHUNKS):
-            pos_k = held.tile([C, CHUNK_TOKENS[k]], F32, name=f"pos{k}", align_bytes=DMA_ALIGN)
-            nc.sync.dma_start(pos_k[:], pos[:, CHUNK_STARTS[k] : CHUNK_STARTS[k] + CHUNK_TOKENS[k]])
-            positions.append(pos_k)
+        for p in range(BLOCKS // PAIR):
+            pos_p = held.tile([C, PAIR * BLOCK], F32, name=f"pos{p}", align_bytes=DMA_ALIGN)
+            nc.sync.dma_start(pos_p[:], pos[:, p * PAIR * BLOCK : (p + 1) * PAIR * BLOCK])
+            positions.append(pos_p)
         weights = held.tile([C, M_BLOCKS * 128], BF16, name="weights")
         nc.sync.dma_start(weights[:], w_attn)
         identity = held.tile([128, 128], F32, name="identity")
@@ -62,56 +65,67 @@ def tile_jtransformer_kernel(tc, embed, pos, ln_w, ln_b, w_attn, b_attn, offs, o
         nc.vector.memset(one[:], 1.0)
         nc.scalar.activation(one[:], one[:], SQRT)
 
-        def look_up(k):
-            start, tokens = CHUNK_STARTS[k], CHUNK_TOKENS[k]
+        stats_tiles = []
+        for p in range(BLOCKS // PAIR):
+            stats_p = held.tile([BLOCK, EPS_COLUMN + 1], F32, name=f"stats{p}")
+            nc.vector.memset(stats_p[:, EPS_COLUMN : EPS_COLUMN + 1], C * EPS * EPS)
+            stats_tiles.append(stats_p)
+
+        def look_up(p):
+            start, tokens = p * PAIR * BLOCK, PAIR * BLOCK
             res = work.tile([C, tokens], F32, name="res", align_bytes=DMA_ALIGN)
             nc.vector.tensor_tensor(
-                res[:], table[:].indirect(offsets[:, start // 16 : (start + tokens) // 16]), positions[k][:], ADD
+                res[:], table[:].indirect(offsets[:, start // 16 : (start + tokens) // 16]), positions[p][:], ADD
             )
             nc.sync.dma_start(out[0:C, start : start + tokens], res[:])
             res_t = psum.tile([BLOCK, tokens], F32, name="res_t", tag="bank")
-            for b in range(tokens // BLOCK):
+            for b in range(PAIR):
                 nc.tensor.transpose(res_t[:, b * C : (b + 1) * C], res[:, b * BLOCK : (b + 1) * BLOCK], identity[:])
             return res_t
 
-        def layer_norm(k, res_t):
-            tokens = CHUNK_TOKENS[k]
-            blocks = tokens // BLOCK
-            stream = res_t[:].rearrange("t (b c) -> t c b", c=C)
-            if blocks == 1:
-                stream = stream.to_broadcast([BLOCK, C, 2])
-            stats = work.tile([BLOCK, 6], F32, name="stats")
-            nc.vector.bn_stats(stats[:], stream)
-            sets = stats[:].rearrange("t (b s) -> t b s", s=3)
+        def layer_norm(p):
+            stats = stats_tiles[p]
+            nc.vector.bn_stats(stats[:, 0:6], res_ts[p][:].rearrange("t (b c) -> t c b", c=C))
 
-            std = work.tile([BLOCK, blocks, 1], F32, name="std")
-            nc.scalar.activation(std[:], sets[:, 0:blocks, 2:3], SQRT, scale=1.0 / C)
-            nc.vector.tensor_scalar_add(std[:], std[:], EPS)
-            inv_std = work.tile([BLOCK, blocks, 1], F32, name="inv_std")
+            std = work.tile([BLOCK, PAIR], F32, name="std")
+            roots = work.tile([BLOCK, PAIR, 2], F32, name="roots")
+            for b in range(PAIR):
+                variance = 3 * b + 2
+                nc.scalar.activation(
+                    roots[:, b, :],
+                    stats[:, variance : EPS_COLUMN + 1 : EPS_COLUMN - variance],
+                    SQRT,
+                    scale=1.0 / C,
+                    accum_out=std[:, b : b + 1],
+                )
+            inv_std = work.tile([BLOCK, PAIR], F32, name="inv_std")
             nc.vector.reciprocal(inv_std[:], std[:])
 
-            normed = work.tile([BLOCK, tokens], F32, name="normed")
-            for b in range(blocks):
+            for b in range(PAIR):
+                normed = work.tile([BLOCK, C], F32, name=f"normed{b}")
                 nc.vector.tensor_scalar(
-                    normed[:, b * C : (b + 1) * C],
-                    res_t[:, b * C : (b + 1) * C],
-                    sets[:, b, 1:2],
-                    inv_std[:, b, :],
+                    normed[:],
+                    res_ts[p][:, b * C : (b + 1) * C],
+                    stats[:, 3 * b + 1 : 3 * b + 2],
+                    inv_std[:, b : b + 1],
                     SUBTRACT,
                     MULT,
                 )
+                normed_blocks.append(normed)
 
-            normed_t = psum.tile([C, tokens], F32, name="normed_t", tag="bank")
+        def turn_back(k):
+            blocks = PIECE_BLOCKS[k]
+            normed_t = psum.tile([C, blocks * BLOCK], F32, name="normed_t", tag="bank")
             for b in range(blocks):
                 nc.tensor.transpose(
-                    normed_t[:, b * BLOCK : (b + 1) * BLOCK], normed[:, b * C : (b + 1) * C], identity[:]
+                    normed_t[:, b * BLOCK : (b + 1) * BLOCK], normed_blocks[PIECE_STARTS[k] + b][:], identity[:]
                 )
-            x = work.tile([C, tokens], BF16, name="x")
+            x = work.tile([C, blocks * BLOCK], BF16, name="x")
             nc.scalar.activation(x[:], normed_t[:], IDENTITY, bias=shift[:], scale=gain[:])
             return x
 
         def project(k, x):
-            start, tokens = CHUNK_STARTS[k], CHUNK_TOKENS[k]
+            start, tokens = PIECE_STARTS[k] * BLOCK, PIECE_BLOCKS[k] * BLOCK
             for m in range(M_BLOCKS):
                 product = psum.tile([128, tokens], F32, name="product", tag="bank")
                 nc.tensor.matmul(product[:], weights[:, m * 128 : (m + 1) * 128], x[:], start=True, stop=True)
@@ -122,10 +136,13 @@ def tile_jtransformer_kernel(tc, embed, pos, ln_w, ln_b, w_attn, b_attn, offs, o
                     nc.vector.tensor_scalar_add(qkv[:], product[:], bias[:, m : m + 1])
                 nc.sync.dma_start(out[C + m * 128 : C + (m + 1) * 128, start : start + tokens], qkv[:])
 
-        res_ts = [look_up(k) for k in range(CHUNKS)]
+        res_ts = [look_up(p) for p in range(BLOCKS // PAIR)]
+        normed_blocks = []
         xs = []
-        for k in range(CHUNKS + LAG):
-            if k < CHUNKS:
-                xs.append(layer_norm(k, res_ts[k]))
+        for k in range(PIECES + LAG):
+            if k < PIECES:
+                if len(normed_blocks) < PIECE_STARTS[k] + PIECE_BLOCKS[k]:
+                    layer_norm(len(normed_blocks) // PAIR)
+                xs.append(turn_back(k))
             if k >= LAG:
                 project(k - LAG, xs[k - LAG])

@@ -19,6 +19,7 @@ EPS = 1e-5
 BLOCK = 128
 BLOCKS = TOKENS // BLOCK
 PAIR = 2
+PAIRS = BLOCKS // PAIR
 EPS_COLUMN = 8
 PIECE_BLOCKS = [1, 2, 2, 2, 1]
 PIECES = len(PIECE_BLOCKS)
@@ -45,7 +46,7 @@ def tile_jtransformer_kernel(tc, embed, pos, ln_w, ln_b, w_attn, b_attn, offs, o
             words = slice(q * WORDS // TABLE_LOADS, (q + 1) * WORDS // TABLE_LOADS)
             nc.sync.dma_start(table[:, words], embed[:, words])
         positions = []
-        for p in range(BLOCKS // PAIR):
+        for p in range(PAIRS):
             pos_p = held.tile([C, PAIR * BLOCK], F32, name=f"pos{p}", align_bytes=DMA_ALIGN)
             nc.sync.dma_start(pos_p[:], pos[:, p * PAIR * BLOCK : (p + 1) * PAIR * BLOCK])
             positions.append(pos_p)
@@ -66,7 +67,7 @@ def tile_jtransformer_kernel(tc, embed, pos, ln_w, ln_b, w_attn, b_attn, offs, o
         nc.scalar.activation(one[:], one[:], SQRT)
 
         stats_tiles = []
-        for p in range(BLOCKS // PAIR):
+        for p in range(PAIRS):
             stats_p = held.tile([BLOCK, EPS_COLUMN + 1], F32, name=f"stats{p}")
             nc.vector.memset(stats_p[:, EPS_COLUMN : EPS_COLUMN + 1], C * EPS * EPS)
             stats_tiles.append(stats_p)
@@ -83,7 +84,7 @@ def tile_jtransformer_kernel(tc, embed, pos, ln_w, ln_b, w_attn, b_attn, offs, o
                 nc.tensor.transpose(res_t[:, b * C : (b + 1) * C], res[:, b * BLOCK : (b + 1) * BLOCK], identity[:])
             return res_t
 
-        def layer_norm(p):
+        def take_statistics(p):
             stats = stats_tiles[p]
             nc.vector.bn_stats(stats[:, 0:6], res_ts[p][:].rearrange("t (b c) -> t c b", c=C))
 
@@ -100,7 +101,10 @@ def tile_jtransformer_kernel(tc, embed, pos, ln_w, ln_b, w_attn, b_attn, offs, o
                 )
             inv_std = work.tile([BLOCK, PAIR], F32, name="inv_std")
             nc.vector.reciprocal(inv_std[:], std[:])
+            return inv_std
 
+        def normalise(p, inv_std):
+            stats = stats_tiles[p]
             for b in range(PAIR):
                 normed = work.tile([BLOCK, C], F32, name=f"normed{b}")
                 nc.vector.tensor_scalar(
@@ -136,13 +140,20 @@ def tile_jtransformer_kernel(tc, embed, pos, ln_w, ln_b, w_attn, b_attn, offs, o
                     nc.vector.tensor_scalar_add(qkv[:], product[:], bias[:, m : m + 1])
                 nc.sync.dma_start(out[C + m * 128 : C + (m + 1) * 128, start : start + tokens], qkv[:])
 
-        res_ts = [look_up(p) for p in range(BLOCKS // PAIR)]
+        res_ts = [look_up(p) for p in range(PAIRS)]
+        inv_stds = []
         normed_blocks = []
         xs = []
-        for k in range(PIECES + LAG):
-            if k < PIECES:
-                if len(normed_blocks) < PIECE_STARTS[k] + PIECE_BLOCKS[k]:
-                    layer_norm(len(normed_blocks) // PAIR)
-                xs.append(turn_back(k))
-            if k >= LAG:
-                project(k - LAG, xs[k - LAG])
+        for p in range(PAIRS + 1):
+            if p < PAIRS:
+                inv_stds.append(take_statistics(p))
+            if p > 0:
+                normalise(p - 1, inv_stds[p - 1])
+                for k in range(PIECES):
+                    last_block = PIECE_STARTS[k] + PIECE_BLOCKS[k] - 1
+                    if last_block // PAIR == p - 1:
+                        xs.append(turn_back(k))
+                        if k >= LAG:
+                            project(k - LAG, xs[k - LAG])
+        for k in range(PIECES - LAG, PIECES):
+            project(k, xs[k])

@@ -79,14 +79,14 @@ def tile_jtransformer_kernel(tc, embed, pos, ln_w, ln_b, w_attn, b_attn, offs, o
                 res[:], table[:].indirect(offsets[:, start // 16 : (start + tokens) // 16]), positions[p][:], ADD
             )
             nc.sync.dma_start(out[0:C, start : start + tokens], res[:])
-            res_t = psum.tile([BLOCK, tokens], F32, name="res_t", tag="bank")
+            res_t = psum.tile([BLOCK, C, PAIR], F32, name="res_t", tag="bank")
             for b in range(PAIR):
-                nc.tensor.transpose(res_t[:, b * C : (b + 1) * C], res[:, b * BLOCK : (b + 1) * BLOCK], identity[:])
+                nc.tensor.transpose(res_t[:, :, b], res[:, b * BLOCK : (b + 1) * BLOCK], identity[:])
             return res_t
 
         def take_statistics(p):
             stats = stats_tiles[p]
-            nc.vector.bn_stats(stats[:, 0:6], res_ts[p][:].rearrange("t (b c) -> t c b", c=C))
+            nc.vector.bn_stats(stats[:, 0:6], res_ts[p][:].rearrange("t c b -> t (c b)"))
 
             std = work.tile([BLOCK, PAIR], F32, name="std")
             roots = work.tile([BLOCK, PAIR, 2], F32, name="roots")
@@ -109,7 +109,7 @@ def tile_jtransformer_kernel(tc, embed, pos, ln_w, ln_b, w_attn, b_attn, offs, o
                 normed = work.tile([BLOCK, C], F32, name=f"normed{b}")
                 nc.vector.tensor_scalar(
                     normed[:],
-                    res_ts[p][:, b * C : (b + 1) * C],
+                    res_ts[p][:, :, b],
                     stats[:, 3 * b + 1 : 3 * b + 2],
                     inv_std[:, b : b + 1],
                     SUBTRACT,
@@ -141,19 +141,14 @@ def tile_jtransformer_kernel(tc, embed, pos, ln_w, ln_b, w_attn, b_attn, offs, o
                 nc.sync.dma_start(out[C + m * 128 : C + (m + 1) * 128, start : start + tokens], qkv[:])
 
         res_ts = [look_up(p) for p in range(PAIRS)]
-        inv_stds = []
+        inv_stds = [take_statistics(p) for p in range(PAIRS)]
         normed_blocks = []
         xs = []
-        for p in range(PAIRS + 1):
-            if p < PAIRS:
-                inv_stds.append(take_statistics(p))
-            if p > 0:
-                normalise(p - 1, inv_stds[p - 1])
-                for k in range(PIECES):
-                    last_block = PIECE_STARTS[k] + PIECE_BLOCKS[k] - 1
-                    if last_block // PAIR == p - 1:
-                        xs.append(turn_back(k))
-                        if k >= LAG:
-                            project(k - LAG, xs[k - LAG])
-        for k in range(PIECES - LAG, PIECES):
-            project(k, xs[k])
+        for k in range(PIECES + LAG):
+            if k < PIECES:
+                if len(normed_blocks) < PIECE_STARTS[k] + PIECE_BLOCKS[k]:
+                    p = len(normed_blocks) // PAIR
+                    normalise(p, inv_stds[p])
+                xs.append(turn_back(k))
+            if k >= LAG:
+                project(k - LAG, xs[k - LAG])

@@ -20,6 +20,7 @@ BLOCK = 128
 BLOCKS = TOKENS // BLOCK
 PAIR = 2
 PAIRS = BLOCKS // PAIR
+LOOK_UP_BLOCKS = [1, 2, 2, 1]
 EPS_COLUMN = 8
 PIECE_BLOCKS = [1, 2, 2, 2, 1]
 PIECES = len(PIECE_BLOCKS)
@@ -27,7 +28,7 @@ PIECE_STARTS = [sum(PIECE_BLOCKS[:k]) for k in range(PIECES)]
 LAG = 1
 PSUM_BANKS = 8
 DMA_ALIGN = 256
-TABLE_LOADS = 4
+TABLE_LOADS = 2
 
 FLOPS = 2 * C * M_BLOCKS * 128 * TOKENS
 
@@ -48,7 +49,10 @@ def tile_jtransformer_kernel(tc, embed, pos, ln_w, ln_b, w_attn, b_attn, offs, o
         positions = []
         for p in range(PAIRS):
             pos_p = held.tile([C, PAIR * BLOCK], F32, name=f"pos{p}", align_bytes=DMA_ALIGN)
-            nc.sync.dma_start(pos_p[:], pos[:, p * PAIR * BLOCK : (p + 1) * PAIR * BLOCK])
+            step = LOOK_UP_BLOCKS[p] * BLOCK
+            for at in range(0, PAIR * BLOCK, step):
+                start = p * PAIR * BLOCK + at
+                nc.sync.dma_start(pos_p[:, at : at + step], pos[:, start : start + step])
             positions.append(pos_p)
         weights = held.tile([C, M_BLOCKS * 128], BF16, name="weights")
         nc.sync.dma_start(weights[:], w_attn)
@@ -75,9 +79,14 @@ def tile_jtransformer_kernel(tc, embed, pos, ln_w, ln_b, w_attn, b_attn, offs, o
         def look_up(p):
             start, tokens = p * PAIR * BLOCK, PAIR * BLOCK
             res = work.tile([C, tokens], F32, name="res", align_bytes=DMA_ALIGN)
-            nc.vector.tensor_tensor(
-                res[:], table[:].indirect(offsets[:, start // 16 : (start + tokens) // 16]), positions[p][:], ADD
-            )
+            step = LOOK_UP_BLOCKS[p] * BLOCK
+            for at in range(0, tokens, step):
+                nc.vector.tensor_tensor(
+                    res[:, at : at + step],
+                    table[:].indirect(offsets[:, (start + at) // 16 : (start + at + step) // 16]),
+                    positions[p][:, at : at + step],
+                    ADD,
+                )
             nc.sync.dma_start(out[0:C, start : start + tokens], res[:])
             res_t = psum.tile([BLOCK, C, PAIR], F32, name="res_t", tag="bank")
             for b in range(PAIR):

import concourse.mybir as mybir
from concourse.masks import make_identity

F32 = mybir.dt.float32
BF16 = mybir.dt.bfloat16
U16 = mybir.dt.uint16
ADD = mybir.AluOpType.add
SUBTRACT = mybir.AluOpType.subtract
MULT = mybir.AluOpType.mult
SQRT = mybir.ActivationFunctionType.Sqrt
IDENTITY = mybir.ActivationFunctionType.Identity

C = 128
WORDS = 2048
TOKENS = 1024
M_BLOCKS = 3
EPS = 1e-5

BLOCK = 128
BLOCKS = TOKENS // BLOCK
PAIR = 2
PAIRS = BLOCKS // PAIR
LOOK_UP_BLOCKS = [1, 2, 2, 1]
EPS_COLUMN = 8
PIECE_BLOCKS = [1, 2, 2, 2, 1]
PIECES = len(PIECE_BLOCKS)
PIECE_STARTS = [sum(PIECE_BLOCKS[:k]) for k in range(PIECES)]
LAG = 1
PSUM_BANKS = 8
DMA_ALIGN = 256
TABLE_LOADS = 2

FLOPS = 2 * C * M_BLOCKS * 128 * TOKENS


def tile_jtransformer_kernel(tc, embed, pos, ln_w, ln_b, w_attn, b_attn, offs, out):
    nc = tc.nc
    with (
        tc.tile_pool(name="held", bufs=1) as held,
        tc.tile_pool(name="work", bufs=PIECES) as work,
        tc.psum_pool(name="psum", bufs=PSUM_BANKS) as psum,
    ):
        offsets = held.tile([C, TOKENS // 16], U16, name="offsets")
        nc.sync.dma_start(offsets[:], offs)
        table = held.tile([C, WORDS], F32, name="table", align_bytes=DMA_ALIGN)
        for q in range(TABLE_LOADS):
            words = slice(q * WORDS // TABLE_LOADS, (q + 1) * WORDS // TABLE_LOADS)
            nc.sync.dma_start(table[:, words], embed[:, words])
        positions = []
        for p in range(PAIRS):
            pos_p = held.tile([C, PAIR * BLOCK], F32, name=f"pos{p}", align_bytes=DMA_ALIGN)
            step = LOOK_UP_BLOCKS[p] * BLOCK
            for at in range(0, PAIR * BLOCK, step):
                start = p * PAIR * BLOCK + at
                nc.sync.dma_start(pos_p[:, at : at + step], pos[:, start : start + step])
            positions.append(pos_p)
        weights = held.tile([C, M_BLOCKS * 128], BF16, name="weights")
        nc.sync.dma_start(weights[:], w_attn)
        identity = held.tile([128, 128], F32, name="identity")
        make_identity(nc, identity[:])
        gain = held.tile([C, 1], F32, name="gain")
        nc.sync.dma_start(gain[:], ln_w)
        shift = held.tile([C, 1], F32, name="shift")
        nc.sync.dma_start(shift[:], ln_b)
        bias = held.tile([128, M_BLOCKS], F32, name="bias")
        with nc.allow_non_contiguous_dma(reason="384 single values, one to a partition and block"):
            nc.sync.dma_start(bias[:], b_attn.rearrange("(m p) one -> p (m one)", p=128))

        one = held.tile([128, 1], F32, name="one")
        nc.vector.memset(one[:], 1.0)
        nc.scalar.activation(one[:], one[:], SQRT)

        stats_tiles = []
        for p in range(PAIRS):
            stats_p = held.tile([BLOCK, EPS_COLUMN + 1], F32, name=f"stats{p}")
            nc.vector.memset(stats_p[:, EPS_COLUMN : EPS_COLUMN + 1], C * EPS * EPS)
            stats_tiles.append(stats_p)

        def look_up(p):
            start, tokens = p * PAIR * BLOCK, PAIR * BLOCK
            res = work.tile([C, tokens], F32, name="res", align_bytes=DMA_ALIGN)
            step = LOOK_UP_BLOCKS[p] * BLOCK
            for at in range(0, tokens, step):
                nc.vector.tensor_tensor(
                    res[:, at : at + step],
                    table[:].indirect(offsets[:, (start + at) // 16 : (start + at + step) // 16]),
                    positions[p][:, at : at + step],
                    ADD,
                )
            nc.sync.dma_start(out[0:C, start : start + tokens], res[:])
            res_t = psum.tile([BLOCK, C, PAIR], F32, name="res_t", tag="bank")
            for b in range(PAIR):
                nc.tensor.transpose(res_t[:, :, b], res[:, b * BLOCK : (b + 1) * BLOCK], identity[:])
            return res_t

        def take_statistics(p):
            stats = stats_tiles[p]
            nc.vector.bn_stats(stats[:, 0:6], res_ts[p][:].rearrange("t c b -> t (c b)"))

            std = work.tile([BLOCK, PAIR], F32, name="std")
            roots = work.tile([BLOCK, PAIR, 2], F32, name="roots")
            for b in range(PAIR):
                variance = 3 * b + 2
                nc.scalar.activation(
                    roots[:, b, :],
                    stats[:, variance : EPS_COLUMN + 1 : EPS_COLUMN - variance],
                    SQRT,
                    scale=1.0 / C,
                    accum_out=std[:, b : b + 1],
                )
            inv_std = work.tile([BLOCK, PAIR], F32, name="inv_std")
            nc.vector.reciprocal(inv_std[:], std[:])
            return inv_std

        def normalise(p, inv_std):
            stats = stats_tiles[p]
            for b in range(PAIR):
                normed = work.tile([BLOCK, C], F32, name=f"normed{b}")
                nc.vector.tensor_scalar(
                    normed[:],
                    res_ts[p][:, :, b],
                    stats[:, 3 * b + 1 : 3 * b + 2],
                    inv_std[:, b : b + 1],
                    SUBTRACT,
                    MULT,
                )
                normed_blocks.append(normed)

        def turn_back(k):
            blocks = PIECE_BLOCKS[k]
            normed_t = psum.tile([C, blocks * BLOCK], F32, name="normed_t", tag="bank")
            for b in range(blocks):
                nc.tensor.transpose(
                    normed_t[:, b * BLOCK : (b + 1) * BLOCK], normed_blocks[PIECE_STARTS[k] + b][:], identity[:]
                )
            x = work.tile([C, blocks * BLOCK], BF16, name="x")
            nc.scalar.activation(x[:], normed_t[:], IDENTITY, bias=shift[:], scale=gain[:])
            return x

        def project(k, x):
            start, tokens = PIECE_STARTS[k] * BLOCK, PIECE_BLOCKS[k] * BLOCK
            for m in range(M_BLOCKS):
                product = psum.tile([128, tokens], F32, name="product", tag="bank")
                nc.tensor.matmul(product[:], weights[:, m * 128 : (m + 1) * 128], x[:], start=True, stop=True)
                qkv = work.tile([128, tokens], F32, name=f"qkv{m}", align_bytes=DMA_ALIGN)
                if (k * M_BLOCKS + m) % 2 == 0:
                    nc.scalar.activation(qkv[:], product[:], IDENTITY, bias=bias[:, m : m + 1])
                else:
                    nc.vector.tensor_scalar_add(qkv[:], product[:], bias[:, m : m + 1])
                nc.sync.dma_start(out[C + m * 128 : C + (m + 1) * 128, start : start + tokens], qkv[:])

        res_ts = [look_up(p) for p in range(PAIRS)]
        inv_stds = [take_statistics(p) for p in range(PAIRS)]
        normed_blocks = []
        xs = []
        for k in range(PIECES + LAG):
            if k < PIECES:
                if len(normed_blocks) < PIECE_STARTS[k] + PIECE_BLOCKS[k]:
                    p = len(normed_blocks) // PAIR
                    normalise(p, inv_stds[p])
                xs.append(turn_back(k))
            if k >= LAG:
                project(k - LAG, xs[k - LAG])
